import numpy as np
import ml_dtypes

BF16 = ml_dtypes.bfloat16


def bf(x):
    return np.asarray(x, np.float32).astype(BF16)


def f32(x):
    return np.asarray(x, np.float32)


def f64(x):
    return np.asarray(x).astype(np.float64)


def striped(idx):
    return np.tile(idx.reshape(-1, 16).T, (8, 1))


CH, BT, S, K, HALF, N = 2, 1024, 256, 9, 128, 4608


def setup_inputs():
    bound = np.sqrt(1.0 / (CH * K))
    x = f32(np.random.standard_normal((CH, BT, S)))
    w = f32(np.random.uniform(-bound, bound, (1, CH * K)))
    idx = np.concatenate([np.random.permutation(S)[:HALF] for _ in range(N // HALF)])
    return {"x": x, "w": w, "offs": striped(idx)}


def reference(x, w, offs):
    idx = offs[:16].T.reshape(-1)
    taps = idx.reshape(CH, K, S)
    xs = f64(x)
    ws = f64(w).reshape(CH, K)
    res = np.zeros((BT, S))
    for c in range(CH):
        for t in range(K):
            res = res + xs[c][:, taps[c, t]] * ws[c, t]
    return res

@@ -1,0 +1,59 @@
+import concourse.mybir as mybir
+from concourse.masks import make_identity
+
+F32 = mybir.dt.float32
+U16 = mybir.dt.uint16
+MULT = mybir.AluOpType.mult
+ADD = mybir.AluOpType.add
+COPY = mybir.ActivationFunctionType.Copy
+
+P = 128
+CH, BT, S, K = 2, 1024, 256, 9
+TAPS = CH * K
+PAIRS = TAPS // 2
+BLOCKS = BT // P
+TAP_COLS = S // 16
+
+FLOPS = 2 * BT * S * TAPS
+
+
+def tile_abc_2d_agnostic_kernel(tc, x, w, offs, out):
+    nc = tc.nc
+    with (
+        tc.tile_pool(name="held", bufs=1) as held,
+        tc.tile_pool(name="images", bufs=3) as images,
+        tc.tile_pool(name="products", bufs=4) as products,
+        tc.tile_pool(name="totals", bufs=2) as totals,
+        tc.psum_pool(name="banks", bufs=2) as banks,
+    ):
+        offsets = held.tile([P, TAPS * TAP_COLS], U16, name="offsets")
+        nc.sync.dma_start(offsets[:], offs)
+        weights = held.tile([P, TAPS], F32, name="weights")
+        nc.scalar.dma_start(weights[:], w.rearrange("o k -> (o k)").partition_broadcast(P))
+        spread = held.tile([P, TAPS, S], F32, name="spread")
+        for k in range(TAPS):
+            nc.scalar.activation(spread[:, k, :], weights[:, k : k + 1].to_broadcast([P, S]), COPY)
+        identity = held.tile([P, P], F32, name="identity")
+        make_identity(nc, identity[:])
+
+        for b in range(BLOCKS):
+            rows = slice(b * P, (b + 1) * P)
+            image = [images.tile([P, S], F32, name=f"image{c}") for c in range(CH)]
+            nc.sync.dma_start(image[0][:], x[0, rows, :])
+            nc.scalar.dma_start(image[1][:], x[1, rows, :])
+
+            bank = banks.tile([P, 2 * S], F32, name="bank")
+            for pair in range(PAIRS):
+                product = products.tile([P, 2 * S], F32, name="product")
+                for half in range(2):
+                    k = 2 * pair + half
+                    picked = image[k // K][:].indirect(offsets[:, k * TAP_COLS : (k + 1) * TAP_COLS])
+                    weight = spread[:, k, :]
+                    nc.vector.tensor_tensor(product[:, half * S : (half + 1) * S], picked, weight, MULT)
+                nc.tensor.matmul(bank[:], identity[:], product[:], start=(pair == 0), stop=(pair == PAIRS - 1))
+
+            halves = totals.tile([P, 2 * S], F32, name="halves")
+            nc.scalar.activation(halves[:], bank[:], COPY)
+            total = totals.tile([P, S], F32, name="total")
+            nc.gpsimd.tensor_tensor(total[:], halves[:, :S], halves[:, S:], ADD)
+            nc.sync.dma_start(out[rows, :], total[:])

@@ -1,5 +1,4 @@
 import concourse.mybir as mybir
-from concourse.masks import make_identity
 
 F32 = mybir.dt.float32
 U16 = mybir.dt.uint16
@@ -10,7 +9,6 @@ COPY = mybir.ActivationFunctionType.Copy
 P = 128
 CH, BT, S, K = 2, 1024, 256, 9
 TAPS = CH * K
-PAIRS = TAPS // 2
 BLOCKS = BT // P
 TAP_COLS = S // 16
 
@@ -22,9 +20,8 @@ def tile_abc_2d_agnostic_kernel(tc, x, w, offs, out):
     with (
         tc.tile_pool(name="held", bufs=1) as held,
         tc.tile_pool(name="images", bufs=3) as images,
-        tc.tile_pool(name="products", bufs=4) as products,
+        tc.tile_pool(name="products", bufs=3) as products,
         tc.tile_pool(name="totals", bufs=2) as totals,
-        tc.psum_pool(name="banks", bufs=2) as banks,
     ):
         offsets = held.tile([P, TAPS * TAP_COLS], U16, name="offsets")
         nc.sync.dma_start(offsets[:], offs)
@@ -33,8 +30,6 @@ def tile_abc_2d_agnostic_kernel(tc, x, w, offs, out):
         spread = held.tile([P, TAPS, S], F32, name="spread")
         for k in range(TAPS):
             nc.scalar.activation(spread[:, k, :], weights[:, k : k + 1].to_broadcast([P, S]), COPY)
-        identity = held.tile([P, P], F32, name="identity")
-        make_identity(nc, identity[:])
 
         for b in range(BLOCKS):
             rows = slice(b * P, (b + 1) * P)
@@ -42,18 +37,14 @@ def tile_abc_2d_agnostic_kernel(tc, x, w, offs, out):
             nc.sync.dma_start(image[0][:], x[0, rows, :])
             nc.scalar.dma_start(image[1][:], x[1, rows, :])
 
-            bank = banks.tile([P, 2 * S], F32, name="bank")
-            for pair in range(PAIRS):
-                product = products.tile([P, 2 * S], F32, name="product")
-                for half in range(2):
-                    k = 2 * pair + half
-                    picked = image[k // K][:].indirect(offsets[:, k * TAP_COLS : (k + 1) * TAP_COLS])
-                    weight = spread[:, k, :]
-                    nc.vector.tensor_tensor(product[:, half * S : (half + 1) * S], picked, weight, MULT)
-                nc.tensor.matmul(bank[:], identity[:], product[:], start=(pair == 0), stop=(pair == PAIRS - 1))
-
-            halves = totals.tile([P, 2 * S], F32, name="halves")
-            nc.scalar.activation(halves[:], bank[:], COPY)
             total = totals.tile([P, S], F32, name="total")
-            nc.gpsimd.tensor_tensor(total[:], halves[:, :S], halves[:, S:], ADD)
+            for k in range(TAPS):
+                picked = image[k // K][:].indirect(offsets[:, k * TAP_COLS : (k + 1) * TAP_COLS])
+                weight = spread[:, k, :]
+                if k == 0:
+                    nc.vector.tensor_tensor(total[:], picked, weight, MULT)
+                else:
+                    product = products.tile([P, S], F32, name="product")
+                    nc.vector.tensor_tensor(product[:], picked, weight, MULT)
+                    nc.vector.tensor_tensor(total[:], total[:], product[:], ADD)
             nc.sync.dma_start(out[rows, :], total[:])

@@ -1,4 +1,5 @@
 import concourse.mybir as mybir
+from concourse.masks import make_identity
 
 F32 = mybir.dt.float32
 U16 = mybir.dt.uint16
@@ -11,7 +12,7 @@ CH, BT, S, K = 2, 1024, 256, 9
 TAPS = CH * K
 BLOCKS = BT // P
 TAP_COLS = S // 16
-
+PAIRS = TAPS // 2
 FLOPS = 2 * BT * S * TAPS
 
 
@@ -20,8 +21,9 @@ def tile_abc_2d_agnostic_kernel(tc, x, w, offs, out):
     with (
         tc.tile_pool(name="held", bufs=1) as held,
         tc.tile_pool(name="images", bufs=3) as images,
-        tc.tile_pool(name="products", bufs=3) as products,
+        tc.tile_pool(name="products", bufs=6) as products,
         tc.tile_pool(name="totals", bufs=2) as totals,
+        tc.psum_pool(name="banks", bufs=2) as banks,
     ):
         offsets = held.tile([P, TAPS * TAP_COLS], U16, name="offsets")
         nc.sync.dma_start(offsets[:], offs)
@@ -30,6 +32,8 @@ def tile_abc_2d_agnostic_kernel(tc, x, w, offs, out):
         spread = held.tile([P, TAPS, S], F32, name="spread")
         for k in range(TAPS):
             nc.scalar.activation(spread[:, k, :], weights[:, k : k + 1].to_broadcast([P, S]), COPY)
+        identity = held.tile([P, P], F32, name="identity")
+        make_identity(nc, identity[:])
 
         for b in range(BLOCKS):
             rows = slice(b * P, (b + 1) * P)
@@ -37,14 +41,22 @@ def tile_abc_2d_agnostic_kernel(tc, x, w, offs, out):
             nc.sync.dma_start(image[0][:], x[0, rows, :])
             nc.scalar.dma_start(image[1][:], x[1, rows, :])
 
+            bank = banks.tile([P, 2 * S], F32, name="bank")
+            for pair in range(PAIRS):
+                product = products.tile([P, 2 * S], F32, name="product")
+                for half in range(2):
+                    k = 2 * pair + half
+                    picked = image[k // K][:].indirect(offsets[:, k * TAP_COLS : (k + 1) * TAP_COLS])
+                    nc.vector.tensor_tensor(product[:, half * S : (half + 1) * S], picked, spread[:, k, :], MULT)
+                if pair % 3 == 0:
+                    kept = product
+                    continue
+                if pair % 3 == 1:
+                    nc.gpsimd.tensor_tensor(product[:], product[:], kept[:], ADD)
+                nc.tensor.matmul(bank[:], identity[:], product[:], start=(pair == 1), stop=(pair == PAIRS - 1))
+
+            halves = totals.tile([P, 2 * S], F32, name="halves")
+            nc.scalar.activation(halves[:], bank[:], COPY)
             total = totals.tile([P, S], F32, name="total")
-            for k in range(TAPS):
-                picked = image[k // K][:].indirect(offsets[:, k * TAP_COLS : (k + 1) * TAP_COLS])
-                weight = spread[:, k, :]
-                if k == 0:
-                    nc.vector.tensor_tensor(total[:], picked, weight, MULT)
-                else:
-                    product = products.tile([P, S], F32, name="product")
-                    nc.vector.tensor_tensor(product[:], picked, weight, MULT)
-                    nc.vector.tensor_tensor(total[:], total[:], product[:], ADD)
+            nc.gpsimd.tensor_tensor(total[:], halves[:, :S], halves[:, S:], ADD)
             nc.sync.dma_start(out[rows, :], total[:])

@@ -4,7 +4,6 @@ from concourse.masks import make_identity
 F32 = mybir.dt.float32
 U16 = mybir.dt.uint16
 MULT = mybir.AluOpType.mult
-ADD = mybir.AluOpType.add
 COPY = mybir.ActivationFunctionType.Copy
 
 P = 128
@@ -12,7 +11,7 @@ CH, BT, S, K = 2, 1024, 256, 9
 TAPS = CH * K
 BLOCKS = BT // P
 TAP_COLS = S // 16
-PAIRS = TAPS // 2
+HALVES = S // P
 FLOPS = 2 * BT * S * TAPS
 
 
@@ -21,7 +20,7 @@ def tile_abc_2d_agnostic_kernel(tc, x, w, offs, out):
     with (
         tc.tile_pool(name="held", bufs=1) as held,
         tc.tile_pool(name="images", bufs=3) as images,
-        tc.tile_pool(name="products", bufs=6) as products,
+        tc.tile_pool(name="products", bufs=4) as products,
         tc.tile_pool(name="totals", bufs=2) as totals,
         tc.psum_pool(name="banks", bufs=2) as banks,
     ):
@@ -41,22 +40,26 @@ def tile_abc_2d_agnostic_kernel(tc, x, w, offs, out):
             nc.sync.dma_start(image[0][:], x[0, rows, :])
             nc.scalar.dma_start(image[1][:], x[1, rows, :])
 
-            bank = banks.tile([P, 2 * S], F32, name="bank")
-            for pair in range(PAIRS):
-                product = products.tile([P, 2 * S], F32, name="product")
-                for half in range(2):
-                    k = 2 * pair + half
-                    picked = image[k // K][:].indirect(offsets[:, k * TAP_COLS : (k + 1) * TAP_COLS])
-                    nc.vector.tensor_tensor(product[:, half * S : (half + 1) * S], picked, spread[:, k, :], MULT)
-                if pair % 3 == 0:
-                    kept = product
-                    continue
-                if pair % 3 == 1:
-                    nc.gpsimd.tensor_tensor(product[:], product[:], kept[:], ADD)
-                nc.tensor.matmul(bank[:], identity[:], product[:], start=(pair == 1), stop=(pair == PAIRS - 1))
+            flipped = [banks.tile([P, P], F32, name=f"flipped{h}") for h in range(HALVES)]
+            for k in range(TAPS):
+                picked = image[k // K][:].indirect(offsets[:, k * TAP_COLS : (k + 1) * TAP_COLS])
+                product = products.tile([P, S], F32, name="product")
+                nc.vector.tensor_tensor(product[:], picked, spread[:, k, :], MULT)
+                for h in range(HALVES):
+                    nc.tensor.matmul(
+                        flipped[h][:],
+                        product[:, h * P : (h + 1) * P],
+                        identity[:],
+                        is_transpose=True,
+                        start=(k == 0),
+                        stop=(k == TAPS - 1),
+                    )
 
-            halves = totals.tile([P, 2 * S], F32, name="halves")
-            nc.scalar.activation(halves[:], bank[:], COPY)
+            upright = banks.tile([P, S], F32, name="upright")
+            for h in range(HALVES):
+                flipped_sum = totals.tile([P, P], F32, name=f"flipped_sum{h}")
+                nc.scalar.activation(flipped_sum[:], flipped[h][:], COPY)
+                nc.tensor.transpose(upright[:, h * P : (h + 1) * P], flipped_sum[:], identity[:])
             total = totals.tile([P, S], F32, name="total")
-            nc.gpsimd.tensor_tensor(total[:], halves[:, :S], halves[:, S:], ADD)
+            nc.scalar.activation(total[:], upright[:], COPY)
             nc.sync.dma_start(out[rows, :], total[:])

@@ -4,6 +4,7 @@ from concourse.masks import make_identity
 F32 = mybir.dt.float32
 U16 = mybir.dt.uint16
 MULT = mybir.AluOpType.mult
+ADD = mybir.AluOpType.add
 COPY = mybir.ActivationFunctionType.Copy
 
 P = 128
@@ -12,6 +13,7 @@ TAPS = CH * K
 BLOCKS = BT // P
 TAP_COLS = S // 16
 HALVES = S // P
+LEFT_TO_VECTOR = 2
 FLOPS = 2 * BT * S * TAPS
 
 
@@ -40,26 +42,38 @@ def tile_abc_2d_agnostic_kernel(tc, x, w, offs, out):
             nc.sync.dma_start(image[0][:], x[0, rows, :])
             nc.scalar.dma_start(image[1][:], x[1, rows, :])
 
+            flipped_taps = TAPS - LEFT_TO_VECTOR if b == BLOCKS - 1 else TAPS
+
             flipped = [banks.tile([P, P], F32, name=f"flipped{h}") for h in range(HALVES)]
+            upright = banks.tile([P, S], F32, name="upright")
+            left = []
             for k in range(TAPS):
                 picked = image[k // K][:].indirect(offsets[:, k * TAP_COLS : (k + 1) * TAP_COLS])
                 product = products.tile([P, S], F32, name="product")
                 nc.vector.tensor_tensor(product[:], picked, spread[:, k, :], MULT)
-                for h in range(HALVES):
-                    nc.tensor.matmul(
-                        flipped[h][:],
-                        product[:, h * P : (h + 1) * P],
-                        identity[:],
-                        is_transpose=True,
-                        start=(k == 0),
-                        stop=(k == TAPS - 1),
-                    )
+                if k < flipped_taps:
+                    for h in range(HALVES):
+                        nc.tensor.matmul(
+                            flipped[h][:],
+                            product[:, h * P : (h + 1) * P],
+                            identity[:],
+                            is_transpose=True,
+                            start=(k == 0),
+                            stop=(k == flipped_taps - 1),
+                        )
+                else:
+                    left.append(product)
+                if k == flipped_taps - 1:
+                    for h in range(HALVES):
+                        flipped_sum = totals.tile([P, P], F32, name=f"flipped_sum{h}")
+                        nc.scalar.activation(flipped_sum[:], flipped[h][:], COPY)
+                        nc.tensor.transpose(upright[:, h * P : (h + 1) * P], flipped_sum[:], identity[:])
 
-            upright = banks.tile([P, S], F32, name="upright")
-            for h in range(HALVES):
-                flipped_sum = totals.tile([P, P], F32, name=f"flipped_sum{h}")
-                nc.scalar.activation(flipped_sum[:], flipped[h][:], COPY)
-                nc.tensor.transpose(upright[:, h * P : (h + 1) * P], flipped_sum[:], identity[:])
             total = totals.tile([P, S], F32, name="total")
-            nc.scalar.activation(total[:], upright[:], COPY)
+            if not left:
+                nc.scalar.activation(total[:], upright[:], COPY)
+            else:
+                left_sum = totals.tile([P, S], F32, name="left_sum")
+                nc.vector.tensor_tensor(left_sum[:], left[0][:], left[1][:], ADD)
+                nc.vector.tensor_tensor(total[:], upright[:], left_sum[:], ADD)
             nc.sync.dma_start(out[rows, :], total[:])

@@ -22,7 +22,7 @@ def tile_abc_2d_agnostic_kernel(tc, x, w, offs, out):
     with (
         tc.tile_pool(name="held", bufs=1) as held,
         tc.tile_pool(name="images", bufs=3) as images,
-        tc.tile_pool(name="products", bufs=4) as products,
+        tc.tile_pool(name="products", bufs=BLOCKS * TAPS) as products,
         tc.tile_pool(name="totals", bufs=2) as totals,
         tc.psum_pool(name="banks", bufs=2) as banks,
     ):

@@ -21,7 +21,7 @@ def tile_abc_2d_agnostic_kernel(tc, x, w, offs, out):
     nc = tc.nc
     with (
         tc.tile_pool(name="held", bufs=1) as held,
-        tc.tile_pool(name="images", bufs=3) as images,
+        tc.tile_pool(name="images", bufs=1) as images,
         tc.tile_pool(name="products", bufs=BLOCKS * TAPS) as products,
         tc.tile_pool(name="totals", bufs=2) as totals,
         tc.psum_pool(name="banks", bufs=2) as banks,

@@ -69,11 +69,15 @@ def tile_abc_2d_agnostic_kernel(tc, x, w, offs, out):
                         nc.scalar.activation(flipped_sum[:], flipped[h][:], COPY)
                         nc.tensor.transpose(upright[:, h * P : (h + 1) * P], flipped_sum[:], identity[:])
 
-            total = totals.tile([P, S], F32, name="total")
             if not left:
+                total = totals.tile([P, S], F32, name="total")
                 nc.scalar.activation(total[:], upright[:], COPY)
+                nc.sync.dma_start(out[rows, :], total[:])
             else:
                 left_sum = totals.tile([P, S], F32, name="left_sum")
                 nc.vector.tensor_tensor(left_sum[:], left[0][:], left[1][:], ADD)
-                nc.vector.tensor_tensor(total[:], upright[:], left_sum[:], ADD)
-            nc.sync.dma_start(out[rows, :], total[:])
+                for h in range(HALVES):
+                    half = slice(h * P, (h + 1) * P)
+                    half_total = totals.tile([P, P], F32, name=f"half_total{h}")
+                    nc.vector.tensor_tensor(half_total[:], upright[:, half], left_sum[:, half], ADD)
+                    nc.sync.dma_start(out[rows, half], half_total[:])

@@ -14,6 +14,7 @@ BLOCKS = BT // P
 TAP_COLS = S // 16
 HALVES = S // P
 LEFT_TO_VECTOR = 2
+LAST_PIECES = ((0, 192), (192, 256))
 FLOPS = 2 * BT * S * TAPS
 
 
@@ -46,8 +47,9 @@ def tile_abc_2d_agnostic_kernel(tc, x, w, offs, out):
 
             flipped = [banks.tile([P, P], F32, name=f"flipped{h}") for h in range(HALVES)]
             upright = banks.tile([P, S], F32, name="upright")
-            left = []
             for k in range(TAPS):
+                if b == BLOCKS - 1 and k == TAPS - 1:
+                    break
                 picked = image[k // K][:].indirect(offsets[:, k * TAP_COLS : (k + 1) * TAP_COLS])
                 product = products.tile([P, S], F32, name="product")
                 nc.vector.tensor_tensor(product[:], picked, spread[:, k, :], MULT)
@@ -61,23 +63,25 @@ def tile_abc_2d_agnostic_kernel(tc, x, w, offs, out):
                             start=(k == 0),
                             stop=(k == flipped_taps - 1),
                         )
-                else:
-                    left.append(product)
                 if k == flipped_taps - 1:
                     for h in range(HALVES):
                         flipped_sum = totals.tile([P, P], F32, name=f"flipped_sum{h}")
                         nc.scalar.activation(flipped_sum[:], flipped[h][:], COPY)
                         nc.tensor.transpose(upright[:, h * P : (h + 1) * P], flipped_sum[:], identity[:])
 
-            if not left:
+            if b < BLOCKS - 1:
                 total = totals.tile([P, S], F32, name="total")
                 nc.scalar.activation(total[:], upright[:], COPY)
                 nc.sync.dma_start(out[rows, :], total[:])
-            else:
-                left_sum = totals.tile([P, S], F32, name="left_sum")
-                nc.vector.tensor_tensor(left_sum[:], left[0][:], left[1][:], ADD)
-                for h in range(HALVES):
-                    half = slice(h * P, (h + 1) * P)
-                    half_total = totals.tile([P, P], F32, name=f"half_total{h}")
-                    nc.vector.tensor_tensor(half_total[:], upright[:, half], left_sum[:, half], ADD)
-                    nc.sync.dma_start(out[rows, half], half_total[:])
+
+        k = TAPS - 1
+        for first, end in LAST_PIECES:
+            piece = slice(first, end)
+            piece_offsets = offsets[:, k * TAP_COLS + first // 16 : k * TAP_COLS + end // 16]
+            last_product = totals.tile([P, end - first], F32, name=f"last_product{first}")
+            nc.vector.tensor_tensor(last_product[:], image[CH - 1][:].indirect(piece_offsets), spread[:, k, piece], MULT)
+            left_sum = totals.tile([P, end - first], F32, name=f"left_sum{first}")
+            nc.vector.tensor_tensor(left_sum[:], last_product[:], product[:, piece], ADD)
+            piece_total = totals.tile([P, end - first], F32, name=f"piece_total{first}")
+            nc.vector.tensor_tensor(piece_total[:], upright[:, piece], left_sum[:], ADD)
+            nc.sync.dma_start(out[rows, piece], piece_total[:])

import concourse.mybir as mybir
from concourse.masks import make_identity

F32 = mybir.dt.float32
U16 = mybir.dt.uint16
MULT = mybir.AluOpType.mult
ADD = mybir.AluOpType.add
COPY = mybir.ActivationFunctionType.Copy

P = 128
CH, BT, S, K = 2, 1024, 256, 9
TAPS = CH * K
BLOCKS = BT // P
TAP_COLS = S // 16
HALVES = S // P
LEFT_TO_VECTOR = 2
LAST_PIECES = ((0, 192), (192, 256))
FLOPS = 2 * BT * S * TAPS


def tile_abc_2d_agnostic_kernel(tc, x, w, offs, out):
    nc = tc.nc
    with (
        tc.tile_pool(name="held", bufs=1) as held,
        tc.tile_pool(name="images", bufs=1) as images,
        tc.tile_pool(name="products", bufs=BLOCKS * TAPS) as products,
        tc.tile_pool(name="totals", bufs=2) as totals,
        tc.psum_pool(name="banks", bufs=2) as banks,
    ):
        offsets = held.tile([P, TAPS * TAP_COLS], U16, name="offsets")
        nc.sync.dma_start(offsets[:], offs)
        weights = held.tile([P, TAPS], F32, name="weights")
        nc.scalar.dma_start(weights[:], w.rearrange("o k -> (o k)").partition_broadcast(P))
        spread = held.tile([P, TAPS, S], F32, name="spread")
        for k in range(TAPS):
            nc.scalar.activation(spread[:, k, :], weights[:, k : k + 1].to_broadcast([P, S]), COPY)
        identity = held.tile([P, P], F32, name="identity")
        make_identity(nc, identity[:])

        for b in range(BLOCKS):
            rows = slice(b * P, (b + 1) * P)
            image = [images.tile([P, S], F32, name=f"image{c}") for c in range(CH)]
            nc.sync.dma_start(image[0][:], x[0, rows, :])
            nc.scalar.dma_start(image[1][:], x[1, rows, :])

            flipped_taps = TAPS - LEFT_TO_VECTOR if b == BLOCKS - 1 else TAPS

            flipped = [banks.tile([P, P], F32, name=f"flipped{h}") for h in range(HALVES)]
            upright = banks.tile([P, S], F32, name="upright")
            for k in range(TAPS):
                if b == BLOCKS - 1 and k == TAPS - 1:
                    break
                picked = image[k // K][:].indirect(offsets[:, k * TAP_COLS : (k + 1) * TAP_COLS])
                product = products.tile([P, S], F32, name="product")
                nc.vector.tensor_tensor(product[:], picked, spread[:, k, :], MULT)
                if k < flipped_taps:
                    for h in range(HALVES):
                        nc.tensor.matmul(
                            flipped[h][:],
                            product[:, h * P : (h + 1) * P],
                            identity[:],
                            is_transpose=True,
                            start=(k == 0),
                            stop=(k == flipped_taps - 1),
                        )
                if k == flipped_taps - 1:
                    for h in range(HALVES):
                        flipped_sum = totals.tile([P, P], F32, name=f"flipped_sum{h}")
                        nc.scalar.activation(flipped_sum[:], flipped[h][:], COPY)
                        nc.tensor.transpose(upright[:, h * P : (h + 1) * P], flipped_sum[:], identity[:])

            if b < BLOCKS - 1:
                total = totals.tile([P, S], F32, name="total")
                nc.scalar.activation(total[:], upright[:], COPY)
                nc.sync.dma_start(out[rows, :], total[:])

        k = TAPS - 1
        for first, end in LAST_PIECES:
            piece = slice(first, end)
            piece_offsets = offsets[:, k * TAP_COLS + first // 16 : k * TAP_COLS + end // 16]
            last_product = totals.tile([P, end - first], F32, name=f"last_product{first}")
            nc.vector.tensor_tensor(last_product[:], image[CH - 1][:].indirect(piece_offsets), spread[:, k, piece], MULT)
            left_sum = totals.tile([P, end - first], F32, name=f"left_sum{first}")
            nc.vector.tensor_tensor(left_sum[:], last_product[:], product[:, piece], ADD)
            piece_total = totals.tile([P, end - first], F32, name=f"piece_total{first}")
            nc.vector.tensor_tensor(piece_total[:], upright[:, piece], left_sum[:], ADD)
            nc.sync.dma_start(out[rows, piece], piece_total[:])
